import numpy as np
import ml_dtypes


def mxq(x, axis, fmt="e4m3"):
    dtype, down = {"e4m3": (ml_dtypes.float8_e4m3fn, 7), "e5m2": (ml_dtypes.float8_e5m2, 14)}[fmt]
    v = np.moveaxis(np.asarray(x, np.float32).astype(ml_dtypes.bfloat16).astype(np.float64), axis, -1)
    blocks = v.reshape(v.shape[:-1] + (-1, 32))
    amax = np.abs(blocks).max(-1, keepdims=True)
    byte = np.maximum(np.where(amax > 0, np.frexp(amax)[1] - 1 + 127, 0) - down, 1)
    scale = np.exp2(byte - 127.0)
    codes = (blocks / scale).astype(np.float32).astype(dtype).astype(np.float64)
    return np.moveaxis((codes * scale).reshape(v.shape), -1, axis)


WIDE = False


def mx_kscale(k):
    if not WIDE:
        return np.ones(k)
    levels = np.array([10, -10, 5, -5, 0])
    a = np.random.permutation(np.resize(levels, k // 512 * 4)).reshape(k // 512, 4)
    idx = np.arange(k)
    return np.exp2(a[idx // 512, idx % 128 // 32])


BF16 = ml_dtypes.bfloat16


def bf(x):
    return np.asarray(x, np.float32).astype(BF16)


def f64(x):
    return np.asarray(x).astype(np.float64)


B, C, G, D, H, W = 2, 512, 32, 8, 8, 8
N = D * H * W
EPS = 1e-6


def group_norm(x, gamma, beta):
    xr = x.reshape(B, G, -1)
    mu = xr.mean(-1, keepdims=True)
    var = xr.var(-1, keepdims=True)
    xn = ((xr - mu) / np.sqrt(var + EPS)).reshape(B, C, N)
    return xn * gamma[None, :, None] + beta[None, :, None]


def setup_inputs():
    s = mx_kscale(C)
    sc = np.exp(0.4 * np.random.standard_normal((B, G)))[:, :, None, None, None, None]
    off = np.random.standard_normal((B, G))[:, :, None, None, None, None]
    x = (np.random.standard_normal((B, G, C // G, D, H, W)) * sc + off).reshape(B, C, D, H, W)
    return {"x": bf(x),
            "gamma": bf((1.0 + 0.2 * np.random.standard_normal(C)) * s),
            "beta": bf(0.3 * np.random.standard_normal(C) * s),
            "w0": bf(np.random.standard_normal((C, C)) * 1.5 / np.sqrt(C) / s[None, :]),
            "b0": bf(0.3 * np.random.standard_normal(C)),
            "w1": bf(np.random.standard_normal((C, C)) * 1.5 / np.sqrt(C) / s[None, :]),
            "b1": bf(0.3 * np.random.standard_normal(C)),
            "w2": bf(np.random.standard_normal((C, C)) / np.sqrt(C) / s[None, :]),
            "b2": bf(0.3 * np.random.standard_normal(C))}


def reference(x, gamma, beta, w0, b0, w1, b1, w2, b2):
    h = group_norm(f64(x), f64(gamma), f64(beta))
    hq = mxq(h, 1, "e4m3")
    q = (mxq(f64(w0), 1, "e4m3") @ hq) + f64(b0)[None, :, None]
    k = (mxq(f64(w1), 1, "e4m3") @ hq) + f64(b1)[None, :, None]
    v = (mxq(f64(w2), 1, "e4m3") @ hq) + f64(b2)[None, :, None]
    return q, k, v

@@ -1,0 +1,266 @@
+from contextlib import ExitStack
+
+import concourse.mybir as mybir
+from concourse.masks import make_identity
+
+F32 = mybir.dt.float32
+BF16 = mybir.dt.bfloat16
+U32 = mybir.dt.uint32
+U8 = mybir.dt.uint8
+FP8X4 = mybir.dt.float8_e4m3fn_x4
+ALU = mybir.AluOpType
+ACT = mybir.ActivationFunctionType
+AXIS = mybir.AxisListType
+
+P = 128
+PACK = 4
+BATCH = 2
+CHANNELS = P * PACK
+VOXELS = 512
+GROUP_PARTS = 16 // PACK
+GROUPS_ON_P = P // GROUP_PARTS
+STATS = 6
+CHUNK_STATS = PACK * STATS
+EPS = 1e-6
+WORDS = 2
+SLOT = 16
+HALF = 2
+
+FLOPS = 2 * 3 * BATCH * CHANNELS * CHANNELS * VOXELS
+
+
+def tile_attnblock_pa_kernel(
+    tc, x, gamma, beta, w0, b0, w1, b1, w2, b2, out_0, out_1, out_2
+):
+    nc = tc.nc
+    weights = [w0, w1, w2]
+    outputs = [out_0, out_1, out_2]
+    vectors = [gamma, beta, b0, b1, b2]
+    GAMMA, BETA, BIAS0 = 0, 1, 2
+
+    with ExitStack() as ctx:
+        const = ctx.enter_context(tc.tile_pool(name="const", bufs=1))
+        keep = ctx.enter_context(tc.tile_pool(name="keep", bufs=1))
+        psum_w = ctx.enter_context(tc.psum_pool(name="psum_w", bufs=2))
+        psum_stats = ctx.enter_context(tc.psum_pool(name="psum_stats", bufs=2))
+        psum_out = ctx.enter_context(tc.psum_pool(name="psum_out", bufs=4))
+
+        x_view = x.rearrange("b (p t) d h w -> b p t (d h w)", t=PACK)
+        x_sb = []
+        for b in range(BATCH):
+            x_sb.append(keep.tile([P, PACK, VOXELS], BF16, name="x_sb%d" % b))
+        w_sb = []
+        for w in range(3):
+            w_sb.append(keep.tile([P, PACK * CHANNELS], BF16, name="w_sb%d" % w))
+
+        def load_x(b):
+            for t in range(PACK):
+                nc.sync.dma_start(out=x_sb[b][:, t, :], in_=x_view[b, :, t, :])
+
+        def load_w(w):
+            nc.sync.dma_start(
+                out=w_sb[w][:], in_=weights[w].rearrange("(q j) c -> q (j c)", j=PACK)
+            )
+
+        load_x(0)
+        load_w(0)
+        load_x(1)
+        load_w(1)
+        load_w(2)
+
+        vec_bf = const.tile([P, len(vectors), SLOT], BF16)
+        for v in range(len(vectors)):
+            nc.scalar.dma_start(
+                out=vec_bf[:, v, 0:PACK], in_=vectors[v].rearrange("(p t) -> p t", t=PACK)
+            )
+
+        eps_col = const.tile([P, 1], F32)
+        nc.vector.memset(eps_col[:], EPS)
+        warm = const.tile([P, 1], F32)
+        nc.scalar.activation(out=warm[:], in_=eps_col[:], func=ACT.Sqrt)
+
+        ident = const.tile([P, P], F32)
+        make_identity(nc, ident[:])
+        in_group = const.tile([P, GROUPS_ON_P], F32)
+        nc.vector.tensor_reduce(
+            out=in_group[:],
+            in_=ident[:].rearrange("p (g j) -> p g j", j=GROUP_PARTS),
+            axis=AXIS.X,
+            op=ALU.add,
+        )
+        same_group = const.tile([P, P], F32)
+        nc.vector.tensor_copy(
+            out=same_group[:].rearrange("p (g j) -> p g j", j=GROUP_PARTS),
+            in_=in_group[:].unsqueeze(2).to_broadcast([P, GROUPS_ON_P, GROUP_PARTS]),
+        )
+        member = const.tile([P, GROUP_PARTS], F32)
+        nc.vector.tensor_reduce(
+            out=member[:],
+            in_=ident[:].rearrange("p (g j) -> p j g", j=GROUP_PARTS),
+            axis=AXIS.X,
+            op=ALU.add,
+        )
+        vec = const.tile([P, len(vectors), PACK], F32)
+        nc.vector.tensor_copy(out=vec[:], in_=vec_bf[:, :, 0:PACK])
+
+        h_codes = []
+        h_scales = []
+        for b in range(BATCH):
+            h_codes.append(keep.tile([P, VOXELS], U32, name="h_codes%d" % b, align_bytes=64))
+            h_scales.append(keep.tile([P, VOXELS], U8, name="h_scales%d" % b, align_bytes=64))
+
+        def quantised_norm(b):
+            chunk_stats = keep.tile([P, PACK, STATS], F32, name="chunk_stats%d" % b)
+            for t in range(PACK):
+                nc.vector.bn_stats(out=chunk_stats[:, t, :], in_=x_sb[b][:, t, :])
+            spread = keep.tile([P, GROUP_PARTS, CHUNK_STATS], F32, name="spread%d" % b)
+            nc.vector.tensor_tensor(
+                out=spread[:],
+                in0=member[:].unsqueeze(2).to_broadcast([P, GROUP_PARTS, CHUNK_STATS]),
+                in1=chunk_stats[:]
+                .rearrange("p t s -> p (t s)")
+                .unsqueeze(1)
+                .to_broadcast([P, GROUP_PARTS, CHUNK_STATS]),
+                op=ALU.mult,
+            )
+            gathered = psum_stats.tile([P, GROUP_PARTS * CHUNK_STATS], F32, name="gathered")
+            nc.tensor.matmul(
+                out=gathered[:],
+                lhsT=same_group[:],
+                rhs=spread[:].rearrange("p j s -> p (j s)"),
+                start=True,
+                stop=True,
+            )
+            mean_var = keep.tile([P, 2], F32, name="mean_var%d" % b)
+            nc.vector.bn_aggr(out=mean_var[:], in_=gathered[:])
+            mean = mean_var[:, 0:1]
+            var = mean_var[:, 1:2]
+
+            std = keep.tile([P, 1], F32, name="std%d" % b)
+            nc.scalar.activation(out=std[:], in_=var, func=ACT.Sqrt, bias=eps_col[:, 0:1])
+            neg_mean_gamma = keep.tile([P, PACK], F32, name="neg_mean_gamma%d" % b)
+            nc.vector.tensor_scalar(
+                out=neg_mean_gamma[:],
+                in0=vec[:, GAMMA, :],
+                scalar1=mean,
+                scalar2=-1.0,
+                op0=ALU.mult,
+                op1=ALU.mult,
+            )
+            rstd = keep.tile([P, 1], F32, name="rstd%d" % b)
+            nc.vector.reciprocal(out=rstd[:], in_=std[:])
+            scale = keep.tile([P, PACK], F32, name="scale%d" % b)
+            nc.vector.tensor_scalar(
+                out=scale[:], in0=vec[:, GAMMA, :], scalar1=rstd[:, 0:1], scalar2=None, op0=ALU.mult
+            )
+            shift = keep.tile([P, PACK], F32, name="shift%d" % b)
+            nc.vector.scalar_tensor_tensor(
+                out=shift[:],
+                in0=neg_mean_gamma[:],
+                scalar=rstd[:, 0:1],
+                in1=vec[:, BETA, :],
+                op0=ALU.mult,
+                op1=ALU.add,
+            )
+
+            h_rows = keep.tile([P, PACK, VOXELS], BF16, name="h_rows%d" % b)
+            for t in range(PACK):
+                if t % 2 == 0:
+                    nc.vector.tensor_scalar(
+                        out=h_rows[:, t, :],
+                        in0=x_sb[b][:, t, :],
+                        scalar1=scale[:, t : t + 1],
+                        scalar2=shift[:, t : t + 1],
+                        op0=ALU.mult,
+                        op1=ALU.add,
+                    )
+                else:
+                    nc.scalar.activation(
+                        out=h_rows[:, t, :],
+                        in_=x_sb[b][:, t, :],
+                        func=ACT.Identity,
+                        scale=scale[:, t : t + 1],
+                        bias=shift[:, t : t + 1],
+                    )
+            h_grouped = keep.tile([P, VOXELS, PACK], BF16, name="h_grouped%d" % b, align_bytes=64)
+            nc.vector.tensor_copy(
+                out=h_grouped[:].rearrange("p (c i) t -> p c t i", i=4),
+                in_=h_rows[:].rearrange("p t (c i) -> p c t i", i=4),
+            )
+            nc.vector.quantize_mx(
+                out=h_codes[b][:].bitcast(FP8X4),
+                scales=h_scales[b][:],
+                in_=h_grouped[:].rearrange("p n t -> p (n t)"),
+            )
+
+        w_codes = []
+        w_scales = []
+        for w in range(3):
+            w_codes.append(keep.tile([P, CHANNELS], U32, name="w_codes%d" % w, align_bytes=64))
+            w_scales.append(keep.tile([P, CHANNELS], U8, name="w_scales%d" % w, align_bytes=64))
+
+        def quantised_weight(w):
+            words = (
+                w_sb[w][:]
+                .bitcast(F32)
+                .rearrange("q (j p u) -> q j u p", j=PACK, u=WORDS)
+            )
+            w_grouped = keep.tile([P, PACK * CHANNELS], BF16, name="w_grouped%d" % w, align_bytes=64)
+            grouped_words = (
+                w_grouped[:]
+                .bitcast(F32)
+                .rearrange("p (j q u) -> p j q u", j=PACK, u=WORDS)
+            )
+            for half in range(PACK // HALF):
+                turned = psum_w.tile([P, HALF, WORDS, P], F32, name="turned")
+                for i in range(HALF):
+                    for u in range(WORDS):
+                        nc.tensor.transpose(
+                            out=turned[:, i, u, :],
+                            in_=words[:, half * HALF + i, u, :],
+                            identity=ident[:],
+                        )
+                nc.scalar.copy(
+                    out=grouped_words[:, half * HALF : (half + 1) * HALF, :, :],
+                    in_=turned[:].rearrange("p i u q -> p i q u"),
+                )
+            nc.vector.quantize_mx(
+                out=w_codes[w][:].bitcast(FP8X4), scales=w_scales[w][:], in_=w_grouped[:]
+            )
+
+        def project(b):
+            for w in range(3):
+                out_view = outputs[w].rearrange("b (q j) n -> b q j n", j=PACK)
+                for half in range(PACK // HALF):
+                    result = keep.tile([P, HALF, VOXELS], F32, name="result%d_%d_%d" % (b, w, half))
+                    for i in range(HALF):
+                        j = half * HALF + i
+                        acc = psum_out.tile([P, VOXELS], F32, name="acc")
+                        nc.tensor.matmul_mx(
+                            out=acc[:],
+                            lhsT=w_codes[w][:, j * P : (j + 1) * P].bitcast(FP8X4),
+                            lhsT_scale=w_scales[w][:, j * P : (j + 1) * P],
+                            rhs=h_codes[b][:].bitcast(FP8X4),
+                            rhs_scale=h_scales[b][:],
+                            start=True,
+                            stop=True,
+                        )
+                        bias = vec[:, BIAS0 + w, j : j + 1]
+                        if i % 2 == 0:
+                            nc.scalar.activation(
+                                out=result[:, i, :], in_=acc[:], func=ACT.Identity, bias=bias
+                            )
+                        else:
+                            nc.vector.tensor_scalar(
+                                out=result[:, i, :], in0=acc[:], scalar1=bias, scalar2=None, op0=ALU.add
+                            )
+                    nc.sync.dma_start(
+                        out=out_view[b, :, half * HALF : (half + 1) * HALF, :], in_=result[:]
+                    )
+
+        quantised_norm(0)
+        for w in range(3):
+            quantised_weight(w)
+        quantised_norm(1)
+        project(0)
+        project(1)

@@ -34,50 +34,78 @@ def tile_attnblock_pa_kernel(
 ):
     nc = tc.nc
     weights = [w0, w1, w2]
+    biases = [b0, b1, b2]
     outputs = [out_0, out_1, out_2]
-    vectors = [gamma, beta, b0, b1, b2]
-    GAMMA, BETA, BIAS0 = 0, 1, 2
 
     with ExitStack() as ctx:
         const = ctx.enter_context(tc.tile_pool(name="const", bufs=1))
         keep = ctx.enter_context(tc.tile_pool(name="keep", bufs=1))
         psum_w = ctx.enter_context(tc.psum_pool(name="psum_w", bufs=2))
-        psum_stats = ctx.enter_context(tc.psum_pool(name="psum_stats", bufs=2))
-        psum_out = ctx.enter_context(tc.psum_pool(name="psum_out", bufs=4))
+        psum_stats = ctx.enter_context(tc.psum_pool(name="psum_stats", bufs=1))
+        psum_out = ctx.enter_context(tc.psum_pool(name="psum_out", bufs=5))
+        ctx.enter_context(tc.manual_schedule())
 
-        x_view = x.rearrange("b (p t) d h w -> b p t (d h w)", t=PACK)
         x_sb = []
+        chunk_stats = []
+        mean_var = []
+        rstd = []
+        neg_mean_gamma = []
+        scale = []
+        shift = []
+        h_grouped = []
+        h_codes = []
+        h_scales = []
         for b in range(BATCH):
             x_sb.append(keep.tile([P, PACK, VOXELS], BF16, name="x_sb%d" % b))
+            chunk_stats.append(keep.tile([P, PACK, STATS], F32, name="chunk_stats%d" % b))
+            mean_var.append(keep.tile([P, 2], F32, name="mean_var%d" % b))
+            rstd.append(keep.tile([P, 1], F32, name="rstd%d" % b))
+            neg_mean_gamma.append(keep.tile([P, PACK], F32, name="neg_mean_gamma%d" % b))
+            scale.append(keep.tile([P, PACK], F32, name="scale%d" % b))
+            shift.append(keep.tile([P, PACK], F32, name="shift%d" % b))
+            h_grouped.append(
+                keep.tile([P, VOXELS, PACK], BF16, name="h_grouped%d" % b, align_bytes=64)
+            )
+            h_codes.append(keep.tile([P, VOXELS], U32, name="h_codes%d" % b, align_bytes=64))
+            h_scales.append(keep.tile([P, VOXELS], U8, name="h_scales%d" % b, align_bytes=64))
         w_sb = []
+        w_grouped = []
+        w_codes = []
+        w_scales = []
         for w in range(3):
             w_sb.append(keep.tile([P, PACK * CHANNELS], BF16, name="w_sb%d" % w))
+            w_grouped.append(
+                keep.tile([P, PACK * CHANNELS], BF16, name="w_grouped%d" % w, align_bytes=64)
+            )
+            w_codes.append(keep.tile([P, CHANNELS], U32, name="w_codes%d" % w, align_bytes=64))
+            w_scales.append(keep.tile([P, CHANNELS], U8, name="w_scales%d" % w, align_bytes=64))
 
-        def load_x(b):
-            for t in range(PACK):
-                nc.sync.dma_start(out=x_sb[b][:, t, :], in_=x_view[b, :, t, :])
+        x_view = x.rearrange("b (p t) d h w -> b p t (d h w)", t=PACK)
 
-        def load_w(w):
+        def load_x(b, rows):
+            for t in range(0, PACK, rows):
+                nc.sync.dma_start(out=x_sb[b][:, t : t + rows, :], in_=x_view[b, :, t : t + rows, :])
+
+        def load_vector(slot, vector):
+            nc.scalar.dma_start(out=slot, in_=vector.rearrange("(p t) -> p t", t=PACK))
+
+        norm_bf = const.tile([P, 2, SLOT], BF16)
+        bias_bf = const.tile([P, 3, SLOT], BF16)
+        load_x(0, 1)
+        load_vector(norm_bf[:, 0, 0:PACK], gamma)
+        load_vector(norm_bf[:, 1, 0:PACK], beta)
+        load_x(1, 2)
+        for w in range(3):
             nc.sync.dma_start(
                 out=w_sb[w][:], in_=weights[w].rearrange("(q j) c -> q (j c)", j=PACK)
-            )
-
-        load_x(0)
-        load_w(0)
-        load_x(1)
-        load_w(1)
-        load_w(2)
-
-        vec_bf = const.tile([P, len(vectors), SLOT], BF16)
-        for v in range(len(vectors)):
-            nc.scalar.dma_start(
-                out=vec_bf[:, v, 0:PACK], in_=vectors[v].rearrange("(p t) -> p t", t=PACK)
             )
 
         eps_col = const.tile([P, 1], F32)
         nc.vector.memset(eps_col[:], EPS)
         warm = const.tile([P, 1], F32)
         nc.scalar.activation(out=warm[:], in_=eps_col[:], func=ACT.Sqrt)
+        for w in range(3):
+            load_vector(bias_bf[:, w, 0:PACK], biases[w])
 
         ident = const.tile([P, P], F32)
         make_identity(nc, ident[:])
@@ -100,24 +128,21 @@ def tile_attnblock_pa_kernel(
             axis=AXIS.X,
             op=ALU.add,
         )
-        vec = const.tile([P, len(vectors), PACK], F32)
-        nc.vector.tensor_copy(out=vec[:], in_=vec_bf[:, :, 0:PACK])
+        norm_f = const.tile([P, 2, PACK], F32)
+        gamma_f = norm_f[:, 0, :]
+        beta_f = norm_f[:, 1, :]
+        bias_f = const.tile([P, 3, PACK], F32)
 
-        h_codes = []
-        h_scales = []
-        for b in range(BATCH):
-            h_codes.append(keep.tile([P, VOXELS], U32, name="h_codes%d" % b, align_bytes=64))
-            h_scales.append(keep.tile([P, VOXELS], U8, name="h_scales%d" % b, align_bytes=64))
+        def row_statistics(b, rows):
+            for t in rows:
+                nc.vector.bn_stats(out=chunk_stats[b][:, t, :], in_=x_sb[b][:, t, :])
 
-        def quantised_norm(b):
-            chunk_stats = keep.tile([P, PACK, STATS], F32, name="chunk_stats%d" % b)
-            for t in range(PACK):
-                nc.vector.bn_stats(out=chunk_stats[:, t, :], in_=x_sb[b][:, t, :])
+        def gather_statistics(b):
             spread = keep.tile([P, GROUP_PARTS, CHUNK_STATS], F32, name="spread%d" % b)
             nc.vector.tensor_tensor(
                 out=spread[:],
                 in0=member[:].unsqueeze(2).to_broadcast([P, GROUP_PARTS, CHUNK_STATS]),
-                in1=chunk_stats[:]
+                in1=chunk_stats[b][:]
                 .rearrange("p t s -> p (t s)")
                 .unsqueeze(1)
                 .to_broadcast([P, GROUP_PARTS, CHUNK_STATS]),
@@ -131,85 +156,65 @@ def tile_attnblock_pa_kernel(
                 start=True,
                 stop=True,
             )
-            mean_var = keep.tile([P, 2], F32, name="mean_var%d" % b)
-            nc.vector.bn_aggr(out=mean_var[:], in_=gathered[:])
-            mean = mean_var[:, 0:1]
-            var = mean_var[:, 1:2]
+            return gathered
 
+        def group_std(b, gathered):
+            nc.vector.bn_aggr(out=mean_var[b][:], in_=gathered[:])
             std = keep.tile([P, 1], F32, name="std%d" % b)
-            nc.scalar.activation(out=std[:], in_=var, func=ACT.Sqrt, bias=eps_col[:, 0:1])
-            neg_mean_gamma = keep.tile([P, PACK], F32, name="neg_mean_gamma%d" % b)
+            nc.scalar.activation(
+                out=std[:], in_=mean_var[b][:, 1:2], func=ACT.Sqrt, bias=eps_col[:, 0:1]
+            )
             nc.vector.tensor_scalar(
-                out=neg_mean_gamma[:],
-                in0=vec[:, GAMMA, :],
-                scalar1=mean,
+                out=neg_mean_gamma[b][:],
+                in0=gamma_f,
+                scalar1=mean_var[b][:, 0:1],
                 scalar2=-1.0,
                 op0=ALU.mult,
                 op1=ALU.mult,
             )
-            rstd = keep.tile([P, 1], F32, name="rstd%d" % b)
-            nc.vector.reciprocal(out=rstd[:], in_=std[:])
-            scale = keep.tile([P, PACK], F32, name="scale%d" % b)
+            return std
+
+        def scale_and_shift(b, std):
+            nc.vector.reciprocal(out=rstd[b][:], in_=std[:])
             nc.vector.tensor_scalar(
-                out=scale[:], in0=vec[:, GAMMA, :], scalar1=rstd[:, 0:1], scalar2=None, op0=ALU.mult
+                out=scale[b][:], in0=gamma_f, scalar1=rstd[b][:, 0:1], scalar2=None, op0=ALU.mult
             )
-            shift = keep.tile([P, PACK], F32, name="shift%d" % b)
             nc.vector.scalar_tensor_tensor(
-                out=shift[:],
-                in0=neg_mean_gamma[:],
-                scalar=rstd[:, 0:1],
-                in1=vec[:, BETA, :],
+                out=shift[b][:],
+                in0=neg_mean_gamma[b][:],
+                scalar=rstd[b][:, 0:1],
+                in1=beta_f,
                 op0=ALU.mult,
                 op1=ALU.add,
             )
 
+        def normalise(b):
             h_rows = keep.tile([P, PACK, VOXELS], BF16, name="h_rows%d" % b)
             for t in range(PACK):
-                if t % 2 == 0:
-                    nc.vector.tensor_scalar(
-                        out=h_rows[:, t, :],
-                        in0=x_sb[b][:, t, :],
-                        scalar1=scale[:, t : t + 1],
-                        scalar2=shift[:, t : t + 1],
-                        op0=ALU.mult,
-                        op1=ALU.add,
-                    )
-                else:
-                    nc.scalar.activation(
-                        out=h_rows[:, t, :],
-                        in_=x_sb[b][:, t, :],
-                        func=ACT.Identity,
-                        scale=scale[:, t : t + 1],
-                        bias=shift[:, t : t + 1],
-                    )
-            h_grouped = keep.tile([P, VOXELS, PACK], BF16, name="h_grouped%d" % b, align_bytes=64)
+                nc.vector.tensor_scalar(
+                    out=h_rows[:, t, :],
+                    in0=x_sb[b][:, t, :],
+                    scalar1=scale[b][:, t : t + 1],
+                    scalar2=shift[b][:, t : t + 1],
+                    op0=ALU.mult,
+                    op1=ALU.add,
+                )
             nc.vector.tensor_copy(
-                out=h_grouped[:].rearrange("p (c i) t -> p c t i", i=4),
+                out=h_grouped[b][:].rearrange("p (c i) t -> p c t i", i=4),
                 in_=h_rows[:].rearrange("p t (c i) -> p c t i", i=4),
             )
+
+        def quantise_h(b):
             nc.vector.quantize_mx(
                 out=h_codes[b][:].bitcast(FP8X4),
                 scales=h_scales[b][:],
-                in_=h_grouped[:].rearrange("p n t -> p (n t)"),
+                in_=h_grouped[b][:].rearrange("p n t -> p (n t)"),
             )
 
-        w_codes = []
-        w_scales = []
-        for w in range(3):
-            w_codes.append(keep.tile([P, CHANNELS], U32, name="w_codes%d" % w, align_bytes=64))
-            w_scales.append(keep.tile([P, CHANNELS], U8, name="w_scales%d" % w, align_bytes=64))
-
-        def quantised_weight(w):
-            words = (
-                w_sb[w][:]
-                .bitcast(F32)
-                .rearrange("q (j p u) -> q j u p", j=PACK, u=WORDS)
-            )
-            w_grouped = keep.tile([P, PACK * CHANNELS], BF16, name="w_grouped%d" % w, align_bytes=64)
+        def turn_weight(w):
+            words = w_sb[w][:].bitcast(F32).rearrange("q (j p u) -> q j u p", j=PACK, u=WORDS)
             grouped_words = (
-                w_grouped[:]
-                .bitcast(F32)
-                .rearrange("p (j q u) -> p j q u", j=PACK, u=WORDS)
+                w_grouped[w][:].bitcast(F32).rearrange("p (j q u) -> p j q u", j=PACK, u=WORDS)
             )
             for half in range(PACK // HALF):
                 turned = psum_w.tile([P, HALF, WORDS, P], F32, name="turned")
@@ -224,43 +229,65 @@ def tile_attnblock_pa_kernel(
                     out=grouped_words[:, half * HALF : (half + 1) * HALF, :, :],
                     in_=turned[:].rearrange("p i u q -> p i q u"),
                 )
+
+        def quantise_weight(w):
             nc.vector.quantize_mx(
-                out=w_codes[w][:].bitcast(FP8X4), scales=w_scales[w][:], in_=w_grouped[:]
+                out=w_codes[w][:].bitcast(FP8X4), scales=w_scales[w][:], in_=w_grouped[w][:]
             )
 
-        def project(b):
-            for w in range(3):
-                out_view = outputs[w].rearrange("b (q j) n -> b q j n", j=PACK)
-                for half in range(PACK // HALF):
-                    result = keep.tile([P, HALF, VOXELS], F32, name="result%d_%d_%d" % (b, w, half))
-                    for i in range(HALF):
-                        j = half * HALF + i
-                        acc = psum_out.tile([P, VOXELS], F32, name="acc")
-                        nc.tensor.matmul_mx(
-                            out=acc[:],
-                            lhsT=w_codes[w][:, j * P : (j + 1) * P].bitcast(FP8X4),
-                            lhsT_scale=w_scales[w][:, j * P : (j + 1) * P],
-                            rhs=h_codes[b][:].bitcast(FP8X4),
-                            rhs_scale=h_scales[b][:],
-                            start=True,
-                            stop=True,
-                        )
-                        bias = vec[:, BIAS0 + w, j : j + 1]
-                        if i % 2 == 0:
-                            nc.scalar.activation(
-                                out=result[:, i, :], in_=acc[:], func=ACT.Identity, bias=bias
-                            )
-                        else:
-                            nc.vector.tensor_scalar(
-                                out=result[:, i, :], in0=acc[:], scalar1=bias, scalar2=None, op0=ALU.add
-                            )
-                    nc.sync.dma_start(
-                        out=out_view[b, :, half * HALF : (half + 1) * HALF, :], in_=result[:]
+        def project(b, w, vector_tiles):
+            out_view = outputs[w].rearrange("b (q j) n -> b q j n", j=PACK)
+            for half in range(PACK // HALF):
+                result = keep.tile([P, HALF, VOXELS], F32, name="result%d_%d_%d" % (b, w, half))
+                for i in range(HALF):
+                    j = half * HALF + i
+                    acc = psum_out.tile([P, VOXELS], F32, name="acc")
+                    nc.tensor.matmul_mx(
+                        out=acc[:],
+                        lhsT=w_codes[w][:, j * P : (j + 1) * P].bitcast(FP8X4),
+                        lhsT_scale=w_scales[w][:, j * P : (j + 1) * P],
+                        rhs=h_codes[b][:].bitcast(FP8X4),
+                        rhs_scale=h_scales[b][:],
+                        start=True,
+                        stop=True,
                     )
+                    bias = bias_f[:, w, j : j + 1]
+                    if j in vector_tiles:
+                        nc.vector.tensor_scalar(
+                            out=result[:, i, :], in0=acc[:], scalar1=bias, scalar2=None, op0=ALU.add
+                        )
+                    else:
+                        nc.scalar.activation(
+                            out=result[:, i, :], in_=acc[:], func=ACT.Identity, bias=bias
+                        )
+                nc.sync.dma_start(
+                    out=out_view[b, :, half * HALF : (half + 1) * HALF, :], in_=result[:]
+                )
 
-        quantised_norm(0)
+        row_statistics(0, range(PACK))
+        gathered0 = gather_statistics(0)
+        nc.vector.tensor_copy(out=norm_f[:], in_=norm_bf[:, :, 0:PACK])
+        row_statistics(1, [0])
+        std0 = group_std(0, gathered0)
+        row_statistics(1, [1])
+        scale_and_shift(0, std0)
         for w in range(3):
-            quantised_weight(w)
-        quantised_norm(1)
-        project(0)
-        project(1)
+            turn_weight(w)
+        normalise(0)
+        nc.vector.tensor_copy(out=bias_f[:], in_=bias_bf[:, :, 0:PACK])
+        quantise_weight(0)
+        quantise_h(0)
+
+        project(0, 0, [])
+        row_statistics(1, [2, 3])
+        quantise_weight(1)
+        gathered1 = gather_statistics(1)
+        quantise_weight(2)
+        std1 = group_std(1, gathered1)
+        project(0, 1, [PACK - 1])
+        scale_and_shift(1, std1)
+        normalise(1)
+        project(0, 2, [PACK - 1])
+        quantise_h(1)
+        for w in range(3):
+            project(1, w, [1, 3])

@@ -19,8 +19,8 @@ CHANNELS = P * PACK
 VOXELS = 512
 GROUP_PARTS = 16 // PACK
 GROUPS_ON_P = P // GROUP_PARTS
-STATS = 6
-CHUNK_STATS = PACK * STATS
+TUPLE = 3
+ROW_TUPLES = 1 + 2 * (PACK - 1)
 EPS = 1e-6
 WORDS = 2
 SLOT = 16
@@ -46,7 +46,9 @@ def tile_attnblock_pa_kernel(
         ctx.enter_context(tc.manual_schedule())
 
         x_sb = []
-        chunk_stats = []
+        row_moments = []
+        row_tuples = []
+        part_tuple = []
         mean_var = []
         rstd = []
         neg_mean_gamma = []
@@ -57,7 +59,9 @@ def tile_attnblock_pa_kernel(
         h_scales = []
         for b in range(BATCH):
             x_sb.append(keep.tile([P, PACK, VOXELS], BF16, name="x_sb%d" % b))
-            chunk_stats.append(keep.tile([P, PACK, STATS], F32, name="chunk_stats%d" % b))
+            row_moments.append(keep.tile([P, 2], F32, name="row_moments%d" % b))
+            row_tuples.append(keep.tile([P, ROW_TUPLES, TUPLE], F32, name="row_tuples%d" % b))
+            part_tuple.append(keep.tile([P, TUPLE], F32, name="part_tuple%d" % b))
             mean_var.append(keep.tile([P, 2], F32, name="mean_var%d" % b))
             rstd.append(keep.tile([P, 1], F32, name="rstd%d" % b))
             neg_mean_gamma.append(keep.tile([P, PACK], F32, name="neg_mean_gamma%d" % b))
@@ -82,30 +86,37 @@ def tile_attnblock_pa_kernel(
 
         x_view = x.rearrange("b (p t) d h w -> b p t (d h w)", t=PACK)
 
-        def load_x(b, rows):
-            for t in range(0, PACK, rows):
-                nc.sync.dma_start(out=x_sb[b][:, t : t + rows, :], in_=x_view[b, :, t : t + rows, :])
+        def load_x(b, first, rows):
+            nc.sync.dma_start(
+                out=x_sb[b][:, first : first + rows, :], in_=x_view[b, :, first : first + rows, :]
+            )
 
         def load_vector(slot, vector):
-            nc.scalar.dma_start(out=slot, in_=vector.rearrange("(p t) -> p t", t=PACK))
+            nc.sync.dma_start(out=slot, in_=vector.rearrange("(p t) -> p t", t=PACK))
 
-        norm_bf = const.tile([P, 2, SLOT], BF16)
-        bias_bf = const.tile([P, 3, SLOT], BF16)
-        load_x(0, 1)
-        load_vector(norm_bf[:, 0, 0:PACK], gamma)
-        load_vector(norm_bf[:, 1, 0:PACK], beta)
-        load_x(1, 2)
-        for w in range(3):
+        def load_weight(w):
             nc.sync.dma_start(
                 out=w_sb[w][:], in_=weights[w].rearrange("(q j) c -> q (j c)", j=PACK)
             )
+
+        norm_bf = const.tile([P, 2, SLOT], BF16)
+        bias_bf = const.tile([P, 3, SLOT], BF16)
+        for t in range(PACK):
+            load_x(0, t, 1)
+        load_vector(norm_bf[:, 0, 0:PACK], gamma)
+        load_vector(norm_bf[:, 1, 0:PACK], beta)
+        load_x(1, 0, 2)
+        load_weight(0)
+        load_x(1, 2, 2)
+        load_weight(1)
+        load_weight(2)
+        for w in range(3):
+            load_vector(bias_bf[:, w, 0:PACK], biases[w])
 
         eps_col = const.tile([P, 1], F32)
         nc.vector.memset(eps_col[:], EPS)
         warm = const.tile([P, 1], F32)
         nc.scalar.activation(out=warm[:], in_=eps_col[:], func=ACT.Sqrt)
-        for w in range(3):
-            load_vector(bias_bf[:, w, 0:PACK], biases[w])
 
         ident = const.tile([P, P], F32)
         make_identity(nc, ident[:])
@@ -132,23 +143,52 @@ def tile_attnblock_pa_kernel(
         gamma_f = norm_f[:, 0, :]
         beta_f = norm_f[:, 1, :]
         bias_f = const.tile([P, 3, PACK], F32)
+        nc.gpsimd.tensor_copy(out=norm_f[:], in_=norm_bf[:, :, 0:PACK])
+        nc.gpsimd.tensor_copy(out=bias_f[:], in_=bias_bf[:, :, 0:PACK])
+        for b in range(BATCH):
+            nc.vector.memset(row_tuples[b][:, 0, 0:1], float(VOXELS))
+            nc.vector.memset(part_tuple[b][:, 0:1], 1.0)
+
+        def row_statistics_on_scalar(b):
+            row = x_sb[b][:, 0, :]
+            unused_a = keep.tile([P, VOXELS], BF16, name="unused_a%d" % b)
+            nc.scalar.activation(
+                out=unused_a[:],
+                in_=row,
+                func=ACT.Identity,
+                scale=1.0 / VOXELS,
+                accum_out=row_moments[b][:, 0:1],
+            )
+            unused_b = keep.tile([P, VOXELS], BF16, name="unused_b%d" % b)
+            nc.scalar.activation(
+                out=unused_b[:],
+                in_=row,
+                func=ACT.Square,
+                scale=-1.0,
+                bias=row_moments[b][:, 0:1],
+                accum_out=row_moments[b][:, 1:2],
+            )
 
         def row_statistics(b, rows):
             for t in rows:
-                nc.vector.bn_stats(out=chunk_stats[b][:, t, :], in_=x_sb[b][:, t, :])
+                nc.vector.bn_stats(
+                    out=row_tuples[b][:, 2 * t - 1 : 2 * t + 1, :].rearrange("p a s -> p (a s)"),
+                    in_=x_sb[b][:, t, :],
+                )
 
         def gather_statistics(b):
-            spread = keep.tile([P, GROUP_PARTS, CHUNK_STATS], F32, name="spread%d" % b)
+            nc.vector.tensor_copy(out=row_tuples[b][:, 0, 1:TUPLE], in_=row_moments[b][:])
+            nc.vector.bn_aggr(
+                out=part_tuple[b][:, 1:TUPLE], in_=row_tuples[b][:].rearrange("p a s -> p (a s)")
+            )
+            spread = keep.tile([P, GROUP_PARTS, TUPLE], F32, name="spread%d" % b)
             nc.vector.tensor_tensor(
                 out=spread[:],
-                in0=member[:].unsqueeze(2).to_broadcast([P, GROUP_PARTS, CHUNK_STATS]),
-                in1=chunk_stats[b][:]
-                .rearrange("p t s -> p (t s)")
-                .unsqueeze(1)
-                .to_broadcast([P, GROUP_PARTS, CHUNK_STATS]),
+                in0=member[:].unsqueeze(2).to_broadcast([P, GROUP_PARTS, TUPLE]),
+                in1=part_tuple[b][:].unsqueeze(1).to_broadcast([P, GROUP_PARTS, TUPLE]),
                 op=ALU.mult,
             )
-            gathered = psum_stats.tile([P, GROUP_PARTS * CHUNK_STATS], F32, name="gathered")
+            gathered = psum_stats.tile([P, GROUP_PARTS * TUPLE], F32, name="gathered")
             nc.tensor.matmul(
                 out=gathered[:],
                 lhsT=same_group[:],
@@ -230,17 +270,22 @@ def tile_attnblock_pa_kernel(
                     in_=turned[:].rearrange("p i u q -> p i q u"),
                 )
 
-        def quantise_weight(w):
+        def quantise_weight(w, half):
+            cols = slice(half * HALF * P, (half + 1) * HALF * P)
             nc.vector.quantize_mx(
-                out=w_codes[w][:].bitcast(FP8X4), scales=w_scales[w][:], in_=w_grouped[w][:]
+                out=w_codes[w][:, cols].bitcast(FP8X4),
+                scales=w_scales[w][:, cols],
+                in_=w_grouped[w][:, half * HALF * CHANNELS : (half + 1) * HALF * CHANNELS],
             )
 
-        def project(b, w, vector_tiles):
+        def project(b, w, vector_tiles, per_store):
             out_view = outputs[w].rearrange("b (q j) n -> b q j n", j=PACK)
-            for half in range(PACK // HALF):
-                result = keep.tile([P, HALF, VOXELS], F32, name="result%d_%d_%d" % (b, w, half))
-                for i in range(HALF):
-                    j = half * HALF + i
+            for first in range(0, PACK, per_store):
+                result = keep.tile(
+                    [P, per_store, VOXELS], F32, name="result%d_%d_%d" % (b, w, first)
+                )
+                for i in range(per_store):
+                    j = first + i
                     acc = psum_out.tile([P, VOXELS], F32, name="acc")
                     nc.tensor.matmul_mx(
                         out=acc[:],
@@ -260,34 +305,34 @@ def tile_attnblock_pa_kernel(
                         nc.scalar.activation(
                             out=result[:, i, :], in_=acc[:], func=ACT.Identity, bias=bias
                         )
-                nc.sync.dma_start(
-                    out=out_view[b, :, half * HALF : (half + 1) * HALF, :], in_=result[:]
-                )
+                nc.sync.dma_start(out=out_view[b, :, first : first + per_store, :], in_=result[:])
 
-        row_statistics(0, range(PACK))
+        row_statistics_on_scalar(0)
+        row_statistics_on_scalar(1)
+        row_statistics(0, [1, 2, 3])
         gathered0 = gather_statistics(0)
-        nc.vector.tensor_copy(out=norm_f[:], in_=norm_bf[:, :, 0:PACK])
-        row_statistics(1, [0])
-        std0 = group_std(0, gathered0)
         row_statistics(1, [1])
+        std0 = group_std(0, gathered0)
         scale_and_shift(0, std0)
         for w in range(3):
             turn_weight(w)
         normalise(0)
-        nc.vector.tensor_copy(out=bias_f[:], in_=bias_bf[:, :, 0:PACK])
-        quantise_weight(0)
+        quantise_weight(0, 0)
         quantise_h(0)
+        quantise_weight(0, 1)
 
-        project(0, 0, [])
+        project(0, 0, [], 1)
         row_statistics(1, [2, 3])
-        quantise_weight(1)
         gathered1 = gather_statistics(1)
-        quantise_weight(2)
+        quantise_weight(1, 0)
+        quantise_weight(1, 1)
         std1 = group_std(1, gathered1)
-        project(0, 1, [PACK - 1])
+        quantise_weight(2, 0)
+        quantise_weight(2, 1)
+        project(0, 1, [], 1)
         scale_and_shift(1, std1)
         normalise(1)
-        project(0, 2, [PACK - 1])
+        project(0, 2, [PACK - 1], 1)
         quantise_h(1)
         for w in range(3):
-            project(1, w, [1, 3])
+            project(1, w, [1, 3], HALF)

@@ -116,7 +116,7 @@ def tile_attnblock_pa_kernel(
         eps_col = const.tile([P, 1], F32)
         nc.vector.memset(eps_col[:], EPS)
         warm = const.tile([P, 1], F32)
-        nc.scalar.activation(out=warm[:], in_=eps_col[:], func=ACT.Sqrt)
+        nc.scalar.activation(out=warm[:], in_=eps_col[:], func=ACT.Abs_reciprocal_sqrt)
 
         ident = const.tile([P, P], F32)
         make_identity(nc, ident[:])
@@ -198,11 +198,13 @@ def tile_attnblock_pa_kernel(
             )
             return gathered
 
-        def group_std(b, gathered):
+        def group_inverse_std(b, gathered):
             nc.vector.bn_aggr(out=mean_var[b][:], in_=gathered[:])
-            std = keep.tile([P, 1], F32, name="std%d" % b)
             nc.scalar.activation(
-                out=std[:], in_=mean_var[b][:, 1:2], func=ACT.Sqrt, bias=eps_col[:, 0:1]
+                out=rstd[b][:],
+                in_=mean_var[b][:, 1:2],
+                func=ACT.Abs_reciprocal_sqrt,
+                bias=eps_col[:, 0:1],
             )
             nc.vector.tensor_scalar(
                 out=neg_mean_gamma[b][:],
@@ -212,10 +214,8 @@ def tile_attnblock_pa_kernel(
                 op0=ALU.mult,
                 op1=ALU.mult,
             )
-            return std
 
-        def scale_and_shift(b, std):
-            nc.vector.reciprocal(out=rstd[b][:], in_=std[:])
+        def scale_and_shift(b):
             nc.vector.tensor_scalar(
                 out=scale[b][:], in0=gamma_f, scalar1=rstd[b][:, 0:1], scalar2=None, op0=ALU.mult
             )
@@ -312,8 +312,8 @@ def tile_attnblock_pa_kernel(
         row_statistics(0, [1, 2, 3])
         gathered0 = gather_statistics(0)
         row_statistics(1, [1])
-        std0 = group_std(0, gathered0)
-        scale_and_shift(0, std0)
+        group_inverse_std(0, gathered0)
+        scale_and_shift(0)
         for w in range(3):
             turn_weight(w)
         normalise(0)
@@ -326,11 +326,11 @@ def tile_attnblock_pa_kernel(
         gathered1 = gather_statistics(1)
         quantise_weight(1, 0)
         quantise_weight(1, 1)
-        std1 = group_std(1, gathered1)
+        group_inverse_std(1, gathered1)
         quantise_weight(2, 0)
         quantise_weight(2, 1)
         project(0, 1, [], 1)
-        scale_and_shift(1, std1)
+        scale_and_shift(1)
         normalise(1)
         project(0, 2, [PACK - 1], 1)
         quantise_h(1)

@@ -25,6 +25,8 @@ EPS = 1e-6
 WORDS = 2
 SLOT = 16
 HALF = 2
+WARM_UP = 10
+BETWEEN = 2
 
 FLOPS = 2 * 3 * BATCH * CHANNELS * CHANNELS * VOXELS
 
@@ -148,6 +150,16 @@ def tile_attnblock_pa_kernel(
         for b in range(BATCH):
             nc.vector.memset(row_tuples[b][:, 0, 0:1], float(VOXELS))
             nc.vector.memset(part_tuple[b][:, 0:1], 1.0)
+
+        spare = psum_out.tile([P, VOXELS], F32, name="acc")
+
+        def keep_tensor_busy(times):
+            for i in range(times):
+                nc.tensor.matmul(
+                    out=spare[:, 0:P], lhsT=ident[:], rhs=ident[:], start=True, stop=True
+                )
+
+        keep_tensor_busy(WARM_UP)
 
         def row_statistics_on_scalar(b):
             row = x_sb[b][:, 0, :]
@@ -316,6 +328,8 @@ def tile_attnblock_pa_kernel(
         scale_and_shift(0)
         for w in range(3):
             turn_weight(w)
+            if w < 2:
+                keep_tensor_busy(BETWEEN)
         normalise(0)
         quantise_weight(0, 0)
         quantise_h(0)

@@ -342,11 +342,12 @@ def tile_attnblock_pa_kernel(
         quantise_weight(1, 1)
         group_inverse_std(1, gathered1)
         quantise_weight(2, 0)
-        quantise_weight(2, 1)
         project(0, 1, [], 1)
         scale_and_shift(1)
         normalise(1)
-        project(0, 2, [PACK - 1], 1)
+        quantise_weight(2, 1)
         quantise_h(1)
-        for w in range(3):
+        project(0, 2, [], 1)
+        project(1, 0, [0, 1, 3], HALF)
+        for w in range(1, 3):
             project(1, w, [1, 3], HALF)

@@ -20,7 +20,7 @@ VOXELS = 512
 GROUP_PARTS = 16 // PACK
 GROUPS_ON_P = P // GROUP_PARTS
 TUPLE = 3
-ROW_TUPLES = 1 + 2 * (PACK - 1)
+ROW_TUPLES = [7, 11]
 EPS = 1e-6
 WORDS = 2
 SLOT = 16
@@ -56,19 +56,21 @@ def tile_attnblock_pa_kernel(
         neg_mean_gamma = []
         scale = []
         shift = []
+        h_rows = []
         h_grouped = []
         h_codes = []
         h_scales = []
         for b in range(BATCH):
             x_sb.append(keep.tile([P, PACK, VOXELS], BF16, name="x_sb%d" % b))
             row_moments.append(keep.tile([P, 2], F32, name="row_moments%d" % b))
-            row_tuples.append(keep.tile([P, ROW_TUPLES, TUPLE], F32, name="row_tuples%d" % b))
+            row_tuples.append(keep.tile([P, ROW_TUPLES[b], TUPLE], F32, name="row_tuples%d" % b))
             part_tuple.append(keep.tile([P, TUPLE], F32, name="part_tuple%d" % b))
             mean_var.append(keep.tile([P, 2], F32, name="mean_var%d" % b))
             rstd.append(keep.tile([P, 1], F32, name="rstd%d" % b))
             neg_mean_gamma.append(keep.tile([P, PACK], F32, name="neg_mean_gamma%d" % b))
             scale.append(keep.tile([P, PACK], F32, name="scale%d" % b))
             shift.append(keep.tile([P, PACK], F32, name="shift%d" % b))
+            h_rows.append(keep.tile([P, PACK, VOXELS], BF16, name="h_rows%d" % b))
             h_grouped.append(
                 keep.tile([P, VOXELS, PACK], BF16, name="h_grouped%d" % b, align_bytes=64)
             )
@@ -103,13 +105,13 @@ def tile_attnblock_pa_kernel(
 
         norm_bf = const.tile([P, 2, SLOT], BF16)
         bias_bf = const.tile([P, 3, SLOT], BF16)
-        for t in range(PACK):
+        for t in [1, 0, 2, 3]:
             load_x(0, t, 1)
         load_vector(norm_bf[:, 0, 0:PACK], gamma)
         load_vector(norm_bf[:, 1, 0:PACK], beta)
         load_x(1, 0, 2)
-        load_weight(0)
         load_x(1, 2, 2)
+        load_weight(0)
         load_weight(1)
         load_weight(2)
         for w in range(3):
@@ -181,18 +183,21 @@ def tile_attnblock_pa_kernel(
                 accum_out=row_moments[b][:, 1:2],
             )
 
-        def row_statistics(b, rows):
-            for t in rows:
-                nc.vector.bn_stats(
-                    out=row_tuples[b][:, 2 * t - 1 : 2 * t + 1, :].rearrange("p a s -> p (a s)"),
-                    in_=x_sb[b][:, t, :],
-                )
+        def piece_statistics(b, place, t, first, count):
+            nc.vector.bn_stats(
+                out=row_tuples[b][:, place : place + 2, :].rearrange("p a s -> p (a s)"),
+                in_=x_sb[b][:, t, first : first + count],
+            )
 
-        def gather_statistics(b):
+        def take_scalar_moments(b):
             nc.vector.tensor_copy(out=row_tuples[b][:, 0, 1:TUPLE], in_=row_moments[b][:])
+
+        def partition_statistics(b):
             nc.vector.bn_aggr(
                 out=part_tuple[b][:, 1:TUPLE], in_=row_tuples[b][:].rearrange("p a s -> p (a s)")
             )
+
+        def gather_statistics(b):
             spread = keep.tile([P, GROUP_PARTS, TUPLE], F32, name="spread%d" % b)
             nc.vector.tensor_tensor(
                 out=spread[:],
@@ -218,6 +223,8 @@ def tile_attnblock_pa_kernel(
                 func=ACT.Abs_reciprocal_sqrt,
                 bias=eps_col[:, 0:1],
             )
+
+        def negative_mean_gamma(b):
             nc.vector.tensor_scalar(
                 out=neg_mean_gamma[b][:],
                 in0=gamma_f,
@@ -241,19 +248,20 @@ def tile_attnblock_pa_kernel(
             )
 
         def normalise(b):
-            h_rows = keep.tile([P, PACK, VOXELS], BF16, name="h_rows%d" % b)
             for t in range(PACK):
                 nc.vector.tensor_scalar(
-                    out=h_rows[:, t, :],
+                    out=h_rows[b][:, t, :],
                     in0=x_sb[b][:, t, :],
                     scalar1=scale[b][:, t : t + 1],
                     scalar2=shift[b][:, t : t + 1],
                     op0=ALU.mult,
                     op1=ALU.add,
                 )
+
+        def interleave(b):
             nc.vector.tensor_copy(
                 out=h_grouped[b][:].rearrange("p (c i) t -> p c t i", i=4),
-                in_=h_rows[:].rearrange("p t (c i) -> p c t i", i=4),
+                in_=h_rows[b][:].rearrange("p t (c i) -> p c t i", i=4),
             )
 
         def quantise_h(b):
@@ -290,9 +298,9 @@ def tile_attnblock_pa_kernel(
                 in_=w_grouped[w][:, half * HALF * CHANNELS : (half + 1) * HALF * CHANNELS],
             )
 
-        def project(b, w, vector_tiles, per_store):
+        def project(b, w, tiles, vector_tiles, per_store):
             out_view = outputs[w].rearrange("b (q j) n -> b q j n", j=PACK)
-            for first in range(0, PACK, per_store):
+            for first in range(tiles.start, tiles.stop, per_store):
                 result = keep.tile(
                     [P, per_store, VOXELS], F32, name="result%d_%d_%d" % (b, w, first)
                 )
@@ -321,33 +329,45 @@ def tile_attnblock_pa_kernel(
 
         row_statistics_on_scalar(0)
         row_statistics_on_scalar(1)
-        row_statistics(0, [1, 2, 3])
+        for t in range(1, PACK):
+            piece_statistics(0, 2 * t - 1, t, 0, VOXELS)
+        take_scalar_moments(0)
+        piece_statistics(1, 1, 1, 0, VOXELS // 2)
+        partition_statistics(0)
+        piece_statistics(1, 3, 1, VOXELS // 2, VOXELS // 2)
         gathered0 = gather_statistics(0)
-        row_statistics(1, [1])
+        piece_statistics(1, 5, 2, 0, VOXELS)
         group_inverse_std(0, gathered0)
+        piece_statistics(1, 7, 3, 0, VOXELS // 2)
+        negative_mean_gamma(0)
         scale_and_shift(0)
+        piece_statistics(1, 9, 3, VOXELS // 2, VOXELS // 2)
         for w in range(3):
             turn_weight(w)
             if w < 2:
                 keep_tensor_busy(BETWEEN)
         normalise(0)
         quantise_weight(0, 0)
-        quantise_h(0)
+        interleave(0)
         quantise_weight(0, 1)
+        quantise_h(0)
 
-        project(0, 0, [], 1)
-        row_statistics(1, [2, 3])
-        gathered1 = gather_statistics(1)
+        project(0, 0, range(0, 2), [], 1)
+        take_scalar_moments(1)
         quantise_weight(1, 0)
+        partition_statistics(1)
         quantise_weight(1, 1)
-        group_inverse_std(1, gathered1)
+        gathered1 = gather_statistics(1)
         quantise_weight(2, 0)
-        project(0, 1, [], 1)
+        group_inverse_std(1, gathered1)
+        negative_mean_gamma(1)
+        project(0, 0, range(2, PACK), [], 1)
+        project(0, 1, range(0, PACK), [], 1)
         scale_and_shift(1)
         normalise(1)
+        interleave(1)
         quantise_weight(2, 1)
         quantise_h(1)
-        project(0, 2, [], 1)
-        project(1, 0, [0, 1, 3], HALF)
-        for w in range(1, 3):
-            project(1, w, [1, 3], HALF)
+        project(0, 2, range(0, PACK), [1, 3], 1)
+        for w in range(3):
+            project(1, w, range(0, PACK), [1, 3], HALF)

@@ -25,6 +25,7 @@ EPS = 1e-6
 WORDS = 2
 SLOT = 16
 HALF = 2
+VECTOR_VOXELS = 320
 WARM_UP = 10
 BETWEEN = 2
 
@@ -258,11 +259,14 @@ def tile_attnblock_pa_kernel(
                     op1=ALU.add,
                 )
 
-        def interleave(b):
-            nc.vector.tensor_copy(
-                out=h_grouped[b][:].rearrange("p (c i) t -> p c t i", i=4),
-                in_=h_rows[b][:].rearrange("p t (c i) -> p c t i", i=4),
-            )
+        def interleave(b, engine, first, count):
+            chunks = slice(first // 4, (first + count) // 4)
+            grouped = h_grouped[b][:].rearrange("p (c i) t -> p c t i", i=4)[:, chunks, :, :]
+            rows = h_rows[b][:].rearrange("p t (c i) -> p c t i", i=4)[:, chunks, :, :]
+            if engine == "scalar":
+                nc.scalar.copy(out=grouped, in_=rows)
+            else:
+                nc.vector.tensor_copy(out=grouped, in_=rows)
 
         def quantise_h(b):
             nc.vector.quantize_mx(
@@ -271,13 +275,17 @@ def tile_attnblock_pa_kernel(
                 in_=h_grouped[b][:].rearrange("p n t -> p (n t)"),
             )
 
-        def turn_weight(w):
+        def turn_weight(w, on_scalar):
             words = w_sb[w][:].bitcast(F32).rearrange("q (j p u) -> q j u p", j=PACK, u=WORDS)
             grouped_words = (
                 w_grouped[w][:].bitcast(F32).rearrange("p (j q u) -> p j q u", j=PACK, u=WORDS)
             )
+            copies = []
             for half in range(PACK // HALF):
-                turned = psum_w.tile([P, HALF, WORDS, P], F32, name="turned")
+                if on_scalar:
+                    turned = psum_w.tile([P, HALF, WORDS, P], F32, name="turned")
+                else:
+                    turned = psum_out.tile([P, HALF, WORDS, P], F32, name="acc")
                 for i in range(HALF):
                     for u in range(WORDS):
                         nc.tensor.transpose(
@@ -285,10 +293,15 @@ def tile_attnblock_pa_kernel(
                             in_=words[:, half * HALF + i, u, :],
                             identity=ident[:],
                         )
-                nc.scalar.copy(
-                    out=grouped_words[:, half * HALF : (half + 1) * HALF, :, :],
-                    in_=turned[:].rearrange("p i u q -> p i q u"),
+                pair = (
+                    grouped_words[:, half * HALF : (half + 1) * HALF, :, :],
+                    turned[:].rearrange("p i u q -> p i q u"),
                 )
+                if on_scalar:
+                    nc.scalar.copy(out=pair[0], in_=pair[1])
+                else:
+                    copies.append(pair)
+            return copies
 
         def quantise_weight(w, half):
             cols = slice(half * HALF * P, (half + 1) * HALF * P)
@@ -342,13 +355,15 @@ def tile_attnblock_pa_kernel(
         negative_mean_gamma(0)
         scale_and_shift(0)
         piece_statistics(1, 9, 3, VOXELS // 2, VOXELS // 2)
-        for w in range(3):
-            turn_weight(w)
-            if w < 2:
-                keep_tensor_busy(BETWEEN)
+        turn_weight(0, True)
+        keep_tensor_busy(BETWEEN)
         normalise(0)
+        interleave(0, "scalar", VECTOR_VOXELS, VOXELS - VECTOR_VOXELS)
+        turn_weight(1, True)
+        keep_tensor_busy(BETWEEN)
+        w2_copies = turn_weight(2, False)
         quantise_weight(0, 0)
-        interleave(0)
+        interleave(0, "vector", 0, VECTOR_VOXELS)
         quantise_weight(0, 1)
         quantise_h(0)
 
@@ -358,14 +373,16 @@ def tile_attnblock_pa_kernel(
         partition_statistics(1)
         quantise_weight(1, 1)
         gathered1 = gather_statistics(1)
-        quantise_weight(2, 0)
+        nc.vector.tensor_copy(out=w2_copies[0][0], in_=w2_copies[0][1])
         group_inverse_std(1, gathered1)
         negative_mean_gamma(1)
+        nc.vector.tensor_copy(out=w2_copies[1][0], in_=w2_copies[1][1])
         project(0, 0, range(2, PACK), [], 1)
         project(0, 1, range(0, PACK), [], 1)
         scale_and_shift(1)
+        quantise_weight(2, 0)
         normalise(1)
-        interleave(1)
+        interleave(1, "vector", 0, VOXELS)
         quantise_weight(2, 1)
         quantise_h(1)
         project(0, 2, range(0, PACK), [1, 3], 1)

@@ -43,9 +43,8 @@ def tile_attnblock_pa_kernel(
     with ExitStack() as ctx:
         const = ctx.enter_context(tc.tile_pool(name="const", bufs=1))
         keep = ctx.enter_context(tc.tile_pool(name="keep", bufs=1))
-        psum_w = ctx.enter_context(tc.psum_pool(name="psum_w", bufs=2))
         psum_stats = ctx.enter_context(tc.psum_pool(name="psum_stats", bufs=1))
-        psum_out = ctx.enter_context(tc.psum_pool(name="psum_out", bufs=5))
+        psum = ctx.enter_context(tc.psum_pool(name="psum", bufs=7))
         ctx.enter_context(tc.manual_schedule())
 
         x_sb = []
@@ -154,7 +153,7 @@ def tile_attnblock_pa_kernel(
             nc.vector.memset(row_tuples[b][:, 0, 0:1], float(VOXELS))
             nc.vector.memset(part_tuple[b][:, 0:1], 1.0)
 
-        spare = psum_out.tile([P, VOXELS], F32, name="acc")
+        spare = psum.tile([P, VOXELS], F32, name="bank")
 
         def keep_tensor_busy(times):
             for i in range(times):
@@ -268,11 +267,13 @@ def tile_attnblock_pa_kernel(
             else:
                 nc.vector.tensor_copy(out=grouped, in_=rows)
 
-        def quantise_h(b):
+        def quantise_h(b, first, count):
             nc.vector.quantize_mx(
-                out=h_codes[b][:].bitcast(FP8X4),
-                scales=h_scales[b][:],
-                in_=h_grouped[b][:].rearrange("p n t -> p (n t)"),
+                out=h_codes[b][:, first : first + count].bitcast(FP8X4),
+                scales=h_scales[b][:, first : first + count],
+                in_=h_grouped[b][:].rearrange("p n t -> p (n t)")[
+                    :, first * PACK : (first + count) * PACK
+                ],
             )
 
         def turn_weight(w, on_scalar):
@@ -282,10 +283,7 @@ def tile_attnblock_pa_kernel(
             )
             copies = []
             for half in range(PACK // HALF):
-                if on_scalar:
-                    turned = psum_w.tile([P, HALF, WORDS, P], F32, name="turned")
-                else:
-                    turned = psum_out.tile([P, HALF, WORDS, P], F32, name="acc")
+                turned = psum.tile([P, HALF, WORDS, P], F32, name="bank")
                 for i in range(HALF):
                     for u in range(WORDS):
                         nc.tensor.transpose(
@@ -319,7 +317,7 @@ def tile_attnblock_pa_kernel(
                 )
                 for i in range(per_store):
                     j = first + i
-                    acc = psum_out.tile([P, VOXELS], F32, name="acc")
+                    acc = psum.tile([P, VOXELS], F32, name="bank")
                     nc.tensor.matmul_mx(
                         out=acc[:],
                         lhsT=w_codes[w][:, j * P : (j + 1) * P].bitcast(FP8X4),
@@ -339,6 +337,26 @@ def tile_attnblock_pa_kernel(
                             out=result[:, i, :], in_=acc[:], func=ACT.Identity, bias=bias
                         )
                 nc.sync.dma_start(out=out_view[b, :, first : first + per_store, :], in_=result[:])
+
+        def project_in_halves(b, w, j):
+            out_view = outputs[w].rearrange("b (q j) n -> b q j n", j=PACK)
+            result = keep.tile([P, 1, VOXELS], F32, name="result%d_%d_%d" % (b, w, j))
+            for first in range(0, VOXELS, VOXELS // 2):
+                cols = slice(first, first + VOXELS // 2)
+                acc = psum.tile([P, VOXELS // 2], F32, name="bank")
+                nc.tensor.matmul_mx(
+                    out=acc[:],
+                    lhsT=w_codes[w][:, j * P : (j + 1) * P].bitcast(FP8X4),
+                    lhsT_scale=w_scales[w][:, j * P : (j + 1) * P],
+                    rhs=h_codes[b][:, cols].bitcast(FP8X4),
+                    rhs_scale=h_scales[b][:, cols],
+                    start=True,
+                    stop=True,
+                )
+                nc.scalar.activation(
+                    out=result[:, 0, cols], in_=acc[:], func=ACT.Identity, bias=bias_f[:, w, j : j + 1]
+                )
+            nc.sync.dma_start(out=out_view[b, :, j : j + 1, :], in_=result[:])
 
         row_statistics_on_scalar(0)
         row_statistics_on_scalar(1)
@@ -365,9 +383,11 @@ def tile_attnblock_pa_kernel(
         quantise_weight(0, 0)
         interleave(0, "vector", 0, VECTOR_VOXELS)
         quantise_weight(0, 1)
-        quantise_h(0)
+        quantise_h(0, 0, VOXELS // 2)
+        quantise_h(0, VOXELS // 2, VOXELS // 2)
 
-        project(0, 0, range(0, 2), [], 1)
+        project_in_halves(0, 0, 0)
+        project(0, 0, range(1, 2), [], 1)
         take_scalar_moments(1)
         quantise_weight(1, 0)
         partition_statistics(1)
@@ -384,7 +404,7 @@ def tile_attnblock_pa_kernel(
         normalise(1)
         interleave(1, "vector", 0, VOXELS)
         quantise_weight(2, 1)
-        quantise_h(1)
+        quantise_h(1, 0, VOXELS)
         project(0, 2, range(0, PACK), [1, 3], 1)
         for w in range(3):
             project(1, w, range(0, PACK), [1, 3], HALF)

@@ -407,4 +407,4 @@ def tile_attnblock_pa_kernel(
         quantise_h(1, 0, VOXELS)
         project(0, 2, range(0, PACK), [1, 3], 1)
         for w in range(3):
-            project(1, w, range(0, PACK), [1, 3], HALF)
+            project(1, w, range(0, PACK), [1, 3], PACK)

from contextlib import ExitStack

import concourse.mybir as mybir
from concourse.masks import make_identity

F32 = mybir.dt.float32
BF16 = mybir.dt.bfloat16
U32 = mybir.dt.uint32
U8 = mybir.dt.uint8
FP8X4 = mybir.dt.float8_e4m3fn_x4
ALU = mybir.AluOpType
ACT = mybir.ActivationFunctionType
AXIS = mybir.AxisListType

P = 128
PACK = 4
BATCH = 2
CHANNELS = P * PACK
VOXELS = 512
GROUP_PARTS = 16 // PACK
GROUPS_ON_P = P // GROUP_PARTS
TUPLE = 3
ROW_TUPLES = [7, 11]
EPS = 1e-6
WORDS = 2
SLOT = 16
HALF = 2
VECTOR_VOXELS = 320
WARM_UP = 10
BETWEEN = 2

FLOPS = 2 * 3 * BATCH * CHANNELS * CHANNELS * VOXELS


def tile_attnblock_pa_kernel(
    tc, x, gamma, beta, w0, b0, w1, b1, w2, b2, out_0, out_1, out_2
):
    nc = tc.nc
    weights = [w0, w1, w2]
    biases = [b0, b1, b2]
    outputs = [out_0, out_1, out_2]

    with ExitStack() as ctx:
        const = ctx.enter_context(tc.tile_pool(name="const", bufs=1))
        keep = ctx.enter_context(tc.tile_pool(name="keep", bufs=1))
        psum_stats = ctx.enter_context(tc.psum_pool(name="psum_stats", bufs=1))
        psum = ctx.enter_context(tc.psum_pool(name="psum", bufs=7))
        ctx.enter_context(tc.manual_schedule())

        x_sb = []
        row_moments = []
        row_tuples = []
        part_tuple = []
        mean_var = []
        rstd = []
        neg_mean_gamma = []
        scale = []
        shift = []
        h_rows = []
        h_grouped = []
        h_codes = []
        h_scales = []
        for b in range(BATCH):
            x_sb.append(keep.tile([P, PACK, VOXELS], BF16, name="x_sb%d" % b))
            row_moments.append(keep.tile([P, 2], F32, name="row_moments%d" % b))
            row_tuples.append(keep.tile([P, ROW_TUPLES[b], TUPLE], F32, name="row_tuples%d" % b))
            part_tuple.append(keep.tile([P, TUPLE], F32, name="part_tuple%d" % b))
            mean_var.append(keep.tile([P, 2], F32, name="mean_var%d" % b))
            rstd.append(keep.tile([P, 1], F32, name="rstd%d" % b))
            neg_mean_gamma.append(keep.tile([P, PACK], F32, name="neg_mean_gamma%d" % b))
            scale.append(keep.tile([P, PACK], F32, name="scale%d" % b))
            shift.append(keep.tile([P, PACK], F32, name="shift%d" % b))
            h_rows.append(keep.tile([P, PACK, VOXELS], BF16, name="h_rows%d" % b))
            h_grouped.append(
                keep.tile([P, VOXELS, PACK], BF16, name="h_grouped%d" % b, align_bytes=64)
            )
            h_codes.append(keep.tile([P, VOXELS], U32, name="h_codes%d" % b, align_bytes=64))
            h_scales.append(keep.tile([P, VOXELS], U8, name="h_scales%d" % b, align_bytes=64))
        w_sb = []
        w_grouped = []
        w_codes = []
        w_scales = []
        for w in range(3):
            w_sb.append(keep.tile([P, PACK * CHANNELS], BF16, name="w_sb%d" % w))
            w_grouped.append(
                keep.tile([P, PACK * CHANNELS], BF16, name="w_grouped%d" % w, align_bytes=64)
            )
            w_codes.append(keep.tile([P, CHANNELS], U32, name="w_codes%d" % w, align_bytes=64))
            w_scales.append(keep.tile([P, CHANNELS], U8, name="w_scales%d" % w, align_bytes=64))

        x_view = x.rearrange("b (p t) d h w -> b p t (d h w)", t=PACK)

        def load_x(b, first, rows):
            nc.sync.dma_start(
                out=x_sb[b][:, first : first + rows, :], in_=x_view[b, :, first : first + rows, :]
            )

        def load_vector(slot, vector):
            nc.sync.dma_start(out=slot, in_=vector.rearrange("(p t) -> p t", t=PACK))

        def load_weight(w):
            nc.sync.dma_start(
                out=w_sb[w][:], in_=weights[w].rearrange("(q j) c -> q (j c)", j=PACK)
            )

        norm_bf = const.tile([P, 2, SLOT], BF16)
        bias_bf = const.tile([P, 3, SLOT], BF16)
        for t in [1, 0, 2, 3]:
            load_x(0, t, 1)
        load_vector(norm_bf[:, 0, 0:PACK], gamma)
        load_vector(norm_bf[:, 1, 0:PACK], beta)
        load_x(1, 0, 2)
        load_x(1, 2, 2)
        load_weight(0)
        load_weight(1)
        load_weight(2)
        for w in range(3):
            load_vector(bias_bf[:, w, 0:PACK], biases[w])

        eps_col = const.tile([P, 1], F32)
        nc.vector.memset(eps_col[:], EPS)
        warm = const.tile([P, 1], F32)
        nc.scalar.activation(out=warm[:], in_=eps_col[:], func=ACT.Abs_reciprocal_sqrt)

        ident = const.tile([P, P], F32)
        make_identity(nc, ident[:])
        in_group = const.tile([P, GROUPS_ON_P], F32)
        nc.vector.tensor_reduce(
            out=in_group[:],
            in_=ident[:].rearrange("p (g j) -> p g j", j=GROUP_PARTS),
            axis=AXIS.X,
            op=ALU.add,
        )
        same_group = const.tile([P, P], F32)
        nc.vector.tensor_copy(
            out=same_group[:].rearrange("p (g j) -> p g j", j=GROUP_PARTS),
            in_=in_group[:].unsqueeze(2).to_broadcast([P, GROUPS_ON_P, GROUP_PARTS]),
        )
        member = const.tile([P, GROUP_PARTS], F32)
        nc.vector.tensor_reduce(
            out=member[:],
            in_=ident[:].rearrange("p (g j) -> p j g", j=GROUP_PARTS),
            axis=AXIS.X,
            op=ALU.add,
        )
        norm_f = const.tile([P, 2, PACK], F32)
        gamma_f = norm_f[:, 0, :]
        beta_f = norm_f[:, 1, :]
        bias_f = const.tile([P, 3, PACK], F32)
        nc.gpsimd.tensor_copy(out=norm_f[:], in_=norm_bf[:, :, 0:PACK])
        nc.gpsimd.tensor_copy(out=bias_f[:], in_=bias_bf[:, :, 0:PACK])
        for b in range(BATCH):
            nc.vector.memset(row_tuples[b][:, 0, 0:1], float(VOXELS))
            nc.vector.memset(part_tuple[b][:, 0:1], 1.0)

        spare = psum.tile([P, VOXELS], F32, name="bank")

        def keep_tensor_busy(times):
            for i in range(times):
                nc.tensor.matmul(
                    out=spare[:, 0:P], lhsT=ident[:], rhs=ident[:], start=True, stop=True
                )

        keep_tensor_busy(WARM_UP)

        def row_statistics_on_scalar(b):
            row = x_sb[b][:, 0, :]
            unused_a = keep.tile([P, VOXELS], BF16, name="unused_a%d" % b)
            nc.scalar.activation(
                out=unused_a[:],
                in_=row,
                func=ACT.Identity,
                scale=1.0 / VOXELS,
                accum_out=row_moments[b][:, 0:1],
            )
            unused_b = keep.tile([P, VOXELS], BF16, name="unused_b%d" % b)
            nc.scalar.activation(
                out=unused_b[:],
                in_=row,
                func=ACT.Square,
                scale=-1.0,
                bias=row_moments[b][:, 0:1],
                accum_out=row_moments[b][:, 1:2],
            )

        def piece_statistics(b, place, t, first, count):
            nc.vector.bn_stats(
                out=row_tuples[b][:, place : place + 2, :].rearrange("p a s -> p (a s)"),
                in_=x_sb[b][:, t, first : first + count],
            )

        def take_scalar_moments(b):
            nc.vector.tensor_copy(out=row_tuples[b][:, 0, 1:TUPLE], in_=row_moments[b][:])

        def partition_statistics(b):
            nc.vector.bn_aggr(
                out=part_tuple[b][:, 1:TUPLE], in_=row_tuples[b][:].rearrange("p a s -> p (a s)")
            )

        def gather_statistics(b):
            spread = keep.tile([P, GROUP_PARTS, TUPLE], F32, name="spread%d" % b)
            nc.vector.tensor_tensor(
                out=spread[:],
                in0=member[:].unsqueeze(2).to_broadcast([P, GROUP_PARTS, TUPLE]),
                in1=part_tuple[b][:].unsqueeze(1).to_broadcast([P, GROUP_PARTS, TUPLE]),
                op=ALU.mult,
            )
            gathered = psum_stats.tile([P, GROUP_PARTS * TUPLE], F32, name="gathered")
            nc.tensor.matmul(
                out=gathered[:],
                lhsT=same_group[:],
                rhs=spread[:].rearrange("p j s -> p (j s)"),
                start=True,
                stop=True,
            )
            return gathered

        def group_inverse_std(b, gathered):
            nc.vector.bn_aggr(out=mean_var[b][:], in_=gathered[:])
            nc.scalar.activation(
                out=rstd[b][:],
                in_=mean_var[b][:, 1:2],
                func=ACT.Abs_reciprocal_sqrt,
                bias=eps_col[:, 0:1],
            )

        def negative_mean_gamma(b):
            nc.vector.tensor_scalar(
                out=neg_mean_gamma[b][:],
                in0=gamma_f,
                scalar1=mean_var[b][:, 0:1],
                scalar2=-1.0,
                op0=ALU.mult,
                op1=ALU.mult,
            )

        def scale_and_shift(b):
            nc.vector.tensor_scalar(
                out=scale[b][:], in0=gamma_f, scalar1=rstd[b][:, 0:1], scalar2=None, op0=ALU.mult
            )
            nc.vector.scalar_tensor_tensor(
                out=shift[b][:],
                in0=neg_mean_gamma[b][:],
                scalar=rstd[b][:, 0:1],
                in1=beta_f,
                op0=ALU.mult,
                op1=ALU.add,
            )

        def normalise(b):
            for t in range(PACK):
                nc.vector.tensor_scalar(
                    out=h_rows[b][:, t, :],
                    in0=x_sb[b][:, t, :],
                    scalar1=scale[b][:, t : t + 1],
                    scalar2=shift[b][:, t : t + 1],
                    op0=ALU.mult,
                    op1=ALU.add,
                )

        def interleave(b, engine, first, count):
            chunks = slice(first // 4, (first + count) // 4)
            grouped = h_grouped[b][:].rearrange("p (c i) t -> p c t i", i=4)[:, chunks, :, :]
            rows = h_rows[b][:].rearrange("p t (c i) -> p c t i", i=4)[:, chunks, :, :]
            if engine == "scalar":
                nc.scalar.copy(out=grouped, in_=rows)
            else:
                nc.vector.tensor_copy(out=grouped, in_=rows)

        def quantise_h(b, first, count):
            nc.vector.quantize_mx(
                out=h_codes[b][:, first : first + count].bitcast(FP8X4),
                scales=h_scales[b][:, first : first + count],
                in_=h_grouped[b][:].rearrange("p n t -> p (n t)")[
                    :, first * PACK : (first + count) * PACK
                ],
            )

        def turn_weight(w, on_scalar):
            words = w_sb[w][:].bitcast(F32).rearrange("q (j p u) -> q j u p", j=PACK, u=WORDS)
            grouped_words = (
                w_grouped[w][:].bitcast(F32).rearrange("p (j q u) -> p j q u", j=PACK, u=WORDS)
            )
            copies = []
            for half in range(PACK // HALF):
                turned = psum.tile([P, HALF, WORDS, P], F32, name="bank")
                for i in range(HALF):
                    for u in range(WORDS):
                        nc.tensor.transpose(
                            out=turned[:, i, u, :],
                            in_=words[:, half * HALF + i, u, :],
                            identity=ident[:],
                        )
                pair = (
                    grouped_words[:, half * HALF : (half + 1) * HALF, :, :],
                    turned[:].rearrange("p i u q -> p i q u"),
                )
                if on_scalar:
                    nc.scalar.copy(out=pair[0], in_=pair[1])
                else:
                    copies.append(pair)
            return copies

        def quantise_weight(w, half):
            cols = slice(half * HALF * P, (half + 1) * HALF * P)
            nc.vector.quantize_mx(
                out=w_codes[w][:, cols].bitcast(FP8X4),
                scales=w_scales[w][:, cols],
                in_=w_grouped[w][:, half * HALF * CHANNELS : (half + 1) * HALF * CHANNELS],
            )

        def project(b, w, tiles, vector_tiles, per_store):
            out_view = outputs[w].rearrange("b (q j) n -> b q j n", j=PACK)
            for first in range(tiles.start, tiles.stop, per_store):
                result = keep.tile(
                    [P, per_store, VOXELS], F32, name="result%d_%d_%d" % (b, w, first)
                )
                for i in range(per_store):
                    j = first + i
                    acc = psum.tile([P, VOXELS], F32, name="bank")
                    nc.tensor.matmul_mx(
                        out=acc[:],
                        lhsT=w_codes[w][:, j * P : (j + 1) * P].bitcast(FP8X4),
                        lhsT_scale=w_scales[w][:, j * P : (j + 1) * P],
                        rhs=h_codes[b][:].bitcast(FP8X4),
                        rhs_scale=h_scales[b][:],
                        start=True,
                        stop=True,
                    )
                    bias = bias_f[:, w, j : j + 1]
                    if j in vector_tiles:
                        nc.vector.tensor_scalar(
                            out=result[:, i, :], in0=acc[:], scalar1=bias, scalar2=None, op0=ALU.add
                        )
                    else:
                        nc.scalar.activation(
                            out=result[:, i, :], in_=acc[:], func=ACT.Identity, bias=bias
                        )
                nc.sync.dma_start(out=out_view[b, :, first : first + per_store, :], in_=result[:])

        def project_in_halves(b, w, j):
            out_view = outputs[w].rearrange("b (q j) n -> b q j n", j=PACK)
            result = keep.tile([P, 1, VOXELS], F32, name="result%d_%d_%d" % (b, w, j))
            for first in range(0, VOXELS, VOXELS // 2):
                cols = slice(first, first + VOXELS // 2)
                acc = psum.tile([P, VOXELS // 2], F32, name="bank")
                nc.tensor.matmul_mx(
                    out=acc[:],
                    lhsT=w_codes[w][:, j * P : (j + 1) * P].bitcast(FP8X4),
                    lhsT_scale=w_scales[w][:, j * P : (j + 1) * P],
                    rhs=h_codes[b][:, cols].bitcast(FP8X4),
                    rhs_scale=h_scales[b][:, cols],
                    start=True,
                    stop=True,
                )
                nc.scalar.activation(
                    out=result[:, 0, cols], in_=acc[:], func=ACT.Identity, bias=bias_f[:, w, j : j + 1]
                )
            nc.sync.dma_start(out=out_view[b, :, j : j + 1, :], in_=result[:])

        row_statistics_on_scalar(0)
        row_statistics_on_scalar(1)
        for t in range(1, PACK):
            piece_statistics(0, 2 * t - 1, t, 0, VOXELS)
        take_scalar_moments(0)
        piece_statistics(1, 1, 1, 0, VOXELS // 2)
        partition_statistics(0)
        piece_statistics(1, 3, 1, VOXELS // 2, VOXELS // 2)
        gathered0 = gather_statistics(0)
        piece_statistics(1, 5, 2, 0, VOXELS)
        group_inverse_std(0, gathered0)
        piece_statistics(1, 7, 3, 0, VOXELS // 2)
        negative_mean_gamma(0)
        scale_and_shift(0)
        piece_statistics(1, 9, 3, VOXELS // 2, VOXELS // 2)
        turn_weight(0, True)
        keep_tensor_busy(BETWEEN)
        normalise(0)
        interleave(0, "scalar", VECTOR_VOXELS, VOXELS - VECTOR_VOXELS)
        turn_weight(1, True)
        keep_tensor_busy(BETWEEN)
        w2_copies = turn_weight(2, False)
        quantise_weight(0, 0)
        interleave(0, "vector", 0, VECTOR_VOXELS)
        quantise_weight(0, 1)
        quantise_h(0, 0, VOXELS // 2)
        quantise_h(0, VOXELS // 2, VOXELS // 2)

        project_in_halves(0, 0, 0)
        project(0, 0, range(1, 2), [], 1)
        take_scalar_moments(1)
        quantise_weight(1, 0)
        partition_statistics(1)
        quantise_weight(1, 1)
        gathered1 = gather_statistics(1)
        nc.vector.tensor_copy(out=w2_copies[0][0], in_=w2_copies[0][1])
        group_inverse_std(1, gathered1)
        negative_mean_gamma(1)
        nc.vector.tensor_copy(out=w2_copies[1][0], in_=w2_copies[1][1])
        project(0, 0, range(2, PACK), [], 1)
        project(0, 1, range(0, PACK), [], 1)
        scale_and_shift(1)
        quantise_weight(2, 0)
        normalise(1)
        interleave(1, "vector", 0, VOXELS)
        quantise_weight(2, 1)
        quantise_h(1, 0, VOXELS)
        project(0, 2, range(0, PACK), [1, 3], 1)
        for w in range(3):
            project(1, w, range(0, PACK), [1, 3], PACK)
